import numpy as np
import ml_dtypes


def mxq(x, axis, fmt="e4m3"):
    dtype, down = {"e4m3": (ml_dtypes.float8_e4m3fn, 7), "e5m2": (ml_dtypes.float8_e5m2, 14)}[fmt]
    v = np.moveaxis(np.asarray(x, np.float32).astype(ml_dtypes.bfloat16).astype(np.float64), axis, -1)
    blocks = v.reshape(v.shape[:-1] + (-1, 32))
    amax = np.abs(blocks).max(-1, keepdims=True)
    byte = np.maximum(np.where(amax > 0, np.frexp(amax)[1] - 1 + 127, 0) - down, 1)
    scale = np.exp2(byte - 127.0)
    codes = (blocks / scale).astype(np.float32).astype(dtype).astype(np.float64)
    return np.moveaxis((codes * scale).reshape(v.shape), -1, axis)


WIDE = False


def mx_kscale(k):
    if not WIDE:
        return np.ones(k)
    levels = np.array([10, -10, 5, -5, 0])
    if k % 512:
        return np.exp2(np.random.permutation(np.resize(levels, k // 32))).repeat(32)
    a = np.empty((k // 512, 16))
    for p in range(k // 512):
        a[p, :8] = np.random.permutation(np.resize(levels, 8))
        for g in range(8):
            far = levels[np.abs(levels - a[p, g]) >= 10]
            a[p, g + 8] = far[np.random.randint(len(far))]
    return np.exp2(a.ravel()).repeat(32)


BF16 = ml_dtypes.bfloat16


def bf(x):
    return np.asarray(x, np.float32).astype(BF16)


def f64(x):
    return np.asarray(x).astype(np.float64)


B, N, D, WIN = 2, 8192, 128, 512
W = N // WIN
PAD = -1.0
QC = 8.0


def setup_inputs():
    s = np.tile(mx_kscale(WIN), W)
    g = np.exp2(np.round(np.log2(s.mean())))
    q = np.random.standard_normal((B, N, D)) * 1.5
    k = np.random.standard_normal((B, N, D)) * 1.5
    v = np.random.standard_normal((B, N, D))
    q[:, :WIN] -= np.log(g) / np.sqrt(D)
    q[:, :, 0] = -QC
    k[:, :, 0] -= np.log(s) * np.sqrt(D) / QC
    v *= (g / s)[:, None]
    return {"q": bf(q), "k": bf(k), "v": bf(v)}


def reference(q, k, v):
    bq = f64(q).reshape(B, W, WIN, D)
    bk = f64(k).reshape(B, W, WIN, D)
    bv = f64(v).reshape(B, W, WIN, D)
    scale = D ** -0.5
    s_cur = (bq @ bk.transpose(0, 1, 3, 2)) * scale
    s_back = (bq[:, 1:] @ bk[:, :-1].transpose(0, 1, 3, 2)) * scale
    s_pad = np.broadcast_to(PAD * bq[:, :1].sum(-1, keepdims=True) * scale, (B, 1, WIN, WIN))
    s = np.concatenate([np.concatenate([s_pad, s_back], axis=1), s_cur], axis=3)
    e = np.exp(s - s.max(-1, keepdims=True))
    vq = mxq(bv, 2, "e4m3")
    o_cur = mxq(e[:, :, :, WIN:], 3, "e4m3") @ vq
    o_back = mxq(e[:, 1:, :, :WIN], 3, "e4m3") @ vq[:, :-1]
    o_pad = np.broadcast_to(PAD * e[:, :1, :, :WIN].sum(-1, keepdims=True), (B, 1, WIN, D))
    out = (o_cur + np.concatenate([o_pad, o_back], axis=1)) / e.sum(-1, keepdims=True)
    return out.reshape(B, N, D)

@@ -1,0 +1,338 @@
+from contextlib import ExitStack
+
+import concourse.mybir as mybir
+from concourse.masks import make_identity
+
+BF16 = mybir.dt.bfloat16
+F32 = mybir.dt.float32
+U32 = mybir.dt.uint32
+U8 = mybir.dt.uint8
+FP8X4 = mybir.dt.float8_e4m3fn_x4
+ACT = mybir.ActivationFunctionType
+ALU = mybir.AluOpType
+AXIS = mybir.AxisListType
+
+BATCH, SEQ, FEAT, WIN = 2, 8192, 128, 512
+P = 128
+PACK = 4
+WINDOWS_PER_SEQ = SEQ // WIN
+WINDOWS = BATCH * WINDOWS_PER_SEQ
+TILES_PER_WIN = WIN // P
+TILES = WINDOWS * TILES_PER_WIN
+SCALE = FEAT**-0.5
+
+REAL_SCORES = WINDOWS * WIN * 2 * WIN - BATCH * WIN * WIN
+FLOPS = 2 * 2 * FEAT * REAL_SCORES
+
+BACK, CUR = 0, 1
+
+PREP_LEAD = 5
+LOAD_AHEAD = 3
+
+
+def tile_localattention_pa_kernel(tc, q, k, v, out):
+    nc = tc.nc
+    q_rows = q.flatten_outer_dims()
+    k_rows = k.flatten_outer_dims()
+    v_rows = v.flatten_outer_dims()
+    out_rows = out.flatten_outer_dims()
+
+    with ExitStack() as ctx:
+        consts = ctx.enter_context(tc.tile_pool(name="consts", bufs=1))
+        loads = ctx.enter_context(tc.tile_pool(name="loads", bufs=LOAD_AHEAD + 3))
+        feat_major = ctx.enter_context(tc.tile_pool(name="feat_major", bufs=4))
+        v_pool = ctx.enter_context(tc.tile_pool(name="v_pool", bufs=5))
+        work = ctx.enter_context(tc.tile_pool(name="work", bufs=3))
+        small = ctx.enter_context(tc.tile_pool(name="small", bufs=4))
+        v_stage = ctx.enter_context(tc.tile_pool(name="v_stage", bufs=1))
+        s_psum = ctx.enter_context(tc.psum_pool(name="s_psum", bufs=5))
+        t_psum = ctx.enter_context(tc.psum_pool(name="t_psum", bufs=2))
+        o_psum = ctx.enter_context(tc.psum_pool(name="o_psum", bufs=1))
+        ctx.enter_context(tc.manual_schedule())
+
+        ident_bf16 = consts.tile([P, P], BF16)
+        make_identity(nc, ident_bf16[:])
+        ident_f32 = consts.tile([P, P], F32)
+        make_identity(nc, ident_f32[:])
+
+        q_nat, k_nat, v_nat = {}, {}, {}
+        qk_bank, qk_t = {}, {}
+        v_grouped, v_codes, v_scales = {}, {}, {}
+        pad_logit = {}
+        s_bank, row_top, bias, e_rows, row_sums = {}, {}, {}, {}, {}
+        t_bank, e_grouped, e_codes, e_scales = {}, {}, {}, {}
+        o_bank, pad_total, total, inverse = {}, {}, {}, {}
+
+        def has_padding(win):
+            return win % WINDOWS_PER_SEQ == 0
+
+        def halves(win):
+            return (CUR,) if has_padding(win) else (BACK, CUR)
+
+        def load_window(win):
+            rows = slice(win * WIN, (win + 1) * WIN)
+            q_win = loads.tile([P, TILES_PER_WIN, FEAT], BF16)
+            nc.sync.dma_start(
+                out=q_win[:], in_=q_rows[rows, :].rearrange("(p r) d -> p r d", r=TILES_PER_WIN)
+            )
+            k_win = loads.tile([P, 2, 2, FEAT], BF16)
+            nc.sync.dma_start(
+                out=k_win[:], in_=k_rows[rows, :].rearrange("(h y u) d -> y h u d", h=2, u=2)
+            )
+            v_win = loads.tile([P, 2, 2, FEAT], BF16)
+            nc.sync.dma_start(
+                out=v_win[:], in_=v_rows[rows, :].rearrange("(p c u) d -> p c u d", c=2, u=2)
+            )
+            q_nat[win], k_nat[win], v_nat[win] = q_win, k_win, v_win
+
+        def padding_logit(win):
+            q_sum = small.tile([P, TILES_PER_WIN], F32)
+            nc.vector.tensor_reduce(out=q_sum[:], in_=q_nat[win][:], axis=AXIS.X, op=ALU.add)
+            pad_win = small.tile([P, TILES_PER_WIN], F32)
+            nc.vector.tensor_scalar(
+                out=pad_win[:], in0=q_sum[:], scalar1=-1.0, scalar2=None, op0=ALU.mult
+            )
+            pad_logit[win] = pad_win
+
+        def transpose_qk(win):
+            qk_ps = t_psum.tile([P, 2, TILES_PER_WIN, P], BF16, tag="transposed")
+            for r in range(TILES_PER_WIN):
+                nc.tensor.transpose(qk_ps[:, 0, r, :], q_nat[win][:, r, :], ident_bf16[:])
+                u, h = divmod(r, 2)
+                nc.tensor.transpose(qk_ps[:, 1, r, :], k_nat[win][:, h, u, :], ident_bf16[:])
+            qk_bank[win] = qk_ps
+
+        def copy_qk(win):
+            qk_win = feat_major.tile([P, 2, TILES_PER_WIN, P], BF16)
+            nc.vector.tensor_copy(out=qk_win[:], in_=qk_bank[win][:])
+            qk_t[win] = qk_win
+
+        def regroup_v(win):
+            v_group_win = v_stage.tile([P, FEAT, 2, 2], BF16, align_bytes=64)
+            nc.gpsimd.tensor_scalar(
+                out=v_group_win[:],
+                in0=v_nat[win][:].rearrange("p c u d -> p d u c"),
+                scalar1=1.0,
+                scalar2=0.0,
+                op0=ALU.mult,
+                op1=ALU.add,
+            )
+            v_grouped[win] = v_group_win
+
+        def quantise_v(win):
+            v_code_win = v_pool.tile([P, FEAT], U32, align_bytes=64)
+            v_scale_win = v_pool.tile([P, FEAT], U8, align_bytes=64)
+            nc.vector.quantize_mx(
+                out=v_code_win[:].bitcast(FP8X4),
+                scales=v_scale_win[:],
+                in_=v_grouped[win][:].rearrange("p d u c -> p (d u c)"),
+            )
+            v_codes[win], v_scales[win] = v_code_win, v_scale_win
+
+        def scores(i, half):
+            win, r = divmod(i, TILES_PER_WIN)
+            if half not in halves(win):
+                return
+            s_ps = s_psum.tile([P, WIN], F32)
+            nc.tensor.matmul(
+                out=s_ps[:],
+                lhsT=qk_t[win][:, 0, r, :],
+                rhs=qk_t[win - 1 + half][:, 1, :, :].rearrange("d j p -> d (j p)"),
+                start=True,
+                stop=True,
+            )
+            s_bank[i, half] = s_ps
+
+        def row_max(i):
+            win, r = divmod(i, TILES_PER_WIN)
+            top = small.tile([P, 2], F32)
+            for half in halves(win):
+                nc.vector.tensor_reduce(
+                    out=top[:, half : half + 1], in_=s_bank[i, half][:], axis=AXIS.X, op=ALU.max
+                )
+            row_top[i] = top
+
+        def exp_bias(i):
+            win, r = divmod(i, TILES_PER_WIN)
+            other = pad_logit[win][:, r : r + 1] if has_padding(win) else row_top[i][:, BACK : BACK + 1]
+            bias_i = small.tile([P, 1], F32)
+            nc.vector.tensor_scalar(
+                out=bias_i[:],
+                in0=row_top[i][:, CUR : CUR + 1],
+                scalar1=other,
+                scalar2=-SCALE,
+                op0=ALU.max,
+                op1=ALU.mult,
+            )
+            bias[i] = bias_i
+
+        def exponential(i, half):
+            win, r = divmod(i, TILES_PER_WIN)
+            if half == BACK:
+                e_tile = work.tile([P, 2 * WIN], BF16)
+                e_rows[i] = e_tile
+                if r == 0:
+                    sums_win = small.tile([P, TILES_PER_WIN, 2], F32)
+                    row_sums[win] = sums_win
+            if half in halves(win):
+                nc.scalar.activation(
+                    out=e_rows[i][:, half * WIN : (half + 1) * WIN],
+                    in_=s_bank[i, half][:],
+                    func=ACT.Exp,
+                    bias=bias[i][:],
+                    scale=SCALE,
+                    accum_out=row_sums[win][:, r, half : half + 1],
+                )
+            else:
+                nc.scalar.activation(
+                    out=row_sums[win][:, r, half : half + 1],
+                    in_=pad_logit[win][:, r : r + 1],
+                    func=ACT.Exp,
+                    bias=bias[i][:],
+                    scale=SCALE,
+                )
+
+        def transpose_e(i):
+            win = i // TILES_PER_WIN
+            t_ps = t_psum.tile([P, 2, 2, P], F32, tag="transposed")
+            e_words = e_rows[i][:].bitcast(F32)
+            for half in halves(win):
+                for u in range(2):
+                    first = (2 * half + u) * P
+                    nc.tensor.transpose(t_ps[:, half, u, :], e_words[:, first : first + P], ident_f32[:])
+            t_bank[i] = t_ps
+
+        def regroup_e(i):
+            win = i // TILES_PER_WIN
+            grouped = work.tile([P, 2 * P * PACK], BF16, align_bytes=64)
+            dst = grouped[:].bitcast(F32).rearrange("p (h m u) -> p h m u", h=2, u=2)
+            src = t_bank[i][:].rearrange("p h u m -> p h m u")
+            first = halves(win)[0]
+            nc.scalar.copy(out=dst[:, first:, :, :], in_=src[:, first:, :, :])
+            e_grouped[i] = grouped
+
+        def quantise_e(i):
+            win = i // TILES_PER_WIN
+            codes = work.tile([P, 2 * P], U32, align_bytes=64)
+            scales = work.tile([P, 2 * P], U8, align_bytes=64)
+            first = halves(win)[0] * P
+            nc.vector.quantize_mx(
+                out=codes[:, first:].bitcast(FP8X4),
+                scales=scales[:, first:],
+                in_=e_grouped[i][:, first * PACK :],
+            )
+            e_codes[i], e_scales[i] = codes, scales
+
+        def weighted_v(i):
+            win, r = divmod(i, TILES_PER_WIN)
+            if r == 0:
+                o_ps = o_psum.tile([P, TILES_PER_WIN, FEAT], F32)
+                o_bank[win] = o_ps
+            for half in halves(win):
+                queries = slice(half * P, (half + 1) * P)
+                nc.tensor.matmul_mx(
+                    out=o_bank[win][:, r, :],
+                    lhsT=e_codes[i][:, queries].bitcast(FP8X4),
+                    lhsT_scale=e_scales[i][:, queries],
+                    rhs=v_codes[win - 1 + half][:].bitcast(FP8X4),
+                    rhs_scale=v_scales[win - 1 + half][:],
+                    start=(half == halves(win)[0]),
+                    stop=(half == CUR),
+                )
+
+        def sum_rows(win):
+            total_win = small.tile([P, TILES_PER_WIN], F32)
+            if has_padding(win):
+                pad_sum = small.tile([P, TILES_PER_WIN], F32)
+                nc.vector.tensor_scalar(
+                    out=pad_sum[:], in0=row_sums[win][:, :, BACK], scalar1=float(WIN), scalar2=None, op0=ALU.mult
+                )
+                nc.vector.tensor_tensor(
+                    out=total_win[:], in0=pad_sum[:], in1=row_sums[win][:, :, CUR], op=ALU.add
+                )
+                pad_total[win] = pad_sum
+            else:
+                nc.vector.tensor_reduce(out=total_win[:], in_=row_sums[win][:], axis=AXIS.X, op=ALU.add)
+            total[win] = total_win
+
+        def invert_sums(win):
+            inverse_win = small.tile([P, TILES_PER_WIN], F32)
+            nc.vector.reciprocal(out=inverse_win[:], in_=total[win][:])
+            inverse[win] = inverse_win
+
+        def finish(win):
+            o_sb = work.tile([P, TILES_PER_WIN, FEAT], F32)
+            if has_padding(win):
+                for r in range(TILES_PER_WIN):
+                    nc.vector.tensor_scalar(
+                        out=o_sb[:, r, :],
+                        in0=o_bank[win][:, r, :],
+                        scalar1=pad_total[win][:, r : r + 1],
+                        scalar2=inverse[win][:, r : r + 1],
+                        op0=ALU.subtract,
+                        op1=ALU.mult,
+                    )
+            else:
+                nc.vector.tensor_tensor(
+                    out=o_sb[:],
+                    in0=o_bank[win][:],
+                    in1=inverse[win][:].unsqueeze(2).to_broadcast([P, TILES_PER_WIN, FEAT]),
+                    op=ALU.mult,
+                )
+            rows = slice(win * WIN, (win + 1) * WIN)
+            nc.sync.dma_start(
+                out=out_rows[rows, :].rearrange("(p r) d -> p r d", r=TILES_PER_WIN), in_=o_sb[:]
+            )
+
+        def is_tile(i):
+            return 0 <= i < TILES
+
+        def window_starting_at(i):
+            return i // TILES_PER_WIN if is_tile(i) and i % TILES_PER_WIN == 0 else None
+
+        for win in range(LOAD_AHEAD):
+            load_window(win)
+
+        for n in range(-PREP_LEAD, TILES + 3):
+            prep_win = window_starting_at(n + PREP_LEAD)
+            if prep_win is not None and prep_win + LOAD_AHEAD < WINDOWS:
+                load_window(prep_win + LOAD_AHEAD)
+
+            if is_tile(n + 2):
+                scores(n + 2, BACK)
+            if is_tile(n):
+                exponential(n, BACK)
+            if is_tile(n - 3):
+                weighted_v(n - 3)
+            if is_tile(n + 2):
+                scores(n + 2, CUR)
+            if is_tile(n):
+                exponential(n, CUR)
+            if is_tile(n - 1):
+                regroup_e(n - 1)
+            if is_tile(n):
+                transpose_e(n)
+
+            if is_tile(n + 1):
+                row_max(n + 1)
+            if is_tile(n - 2):
+                quantise_e(n - 2)
+            if is_tile(n + 1):
+                exp_bias(n + 1)
+
+            if prep_win is not None and has_padding(prep_win):
+                padding_logit(prep_win)
+            if window_starting_at(n + PREP_LEAD - 1) is not None:
+                copy_qk(window_starting_at(n + PREP_LEAD - 1))
+            if window_starting_at(n - 4) is not None:
+                sum_rows(window_starting_at(n - 4))
+            if window_starting_at(n - 5) is not None:
+                invert_sums(window_starting_at(n - 5))
+            if window_starting_at(n - 6) is not None:
+                finish(window_starting_at(n - 6))
+            if window_starting_at(n + 1) is not None:
+                quantise_v(window_starting_at(n + 1))
+            if window_starting_at(n + 5) is not None:
+                regroup_v(window_starting_at(n + 5))
+            if prep_win is not None:
+                transpose_qk(prep_win)

@@ -156,7 +156,7 @@ def tile_localattention_pa_kernel(tc, q, k, v, out):
             win, r = divmod(i, TILES_PER_WIN)
             other = pad_logit[win][:, r : r + 1] if has_padding(win) else row_top[i][:, BACK : BACK + 1]
             bias_i = small.tile([P, 1], F32)
-            nc.vector.tensor_scalar(
+            nc.gpsimd.tensor_scalar(
                 out=bias_i[:],
                 in0=row_top[i][:, CUR : CUR + 1],
                 scalar1=other,

@@ -26,7 +26,7 @@ FLOPS = 2 * 2 * FEAT * REAL_SCORES
 
 BACK, CUR = 0, 1
 
-PREP_LEAD = 5
+PREP_LEAD = 8
 LOAD_AHEAD = 3
 
 
@@ -39,15 +39,16 @@ def tile_localattention_pa_kernel(tc, q, k, v, out):
 
     with ExitStack() as ctx:
         consts = ctx.enter_context(tc.tile_pool(name="consts", bufs=1))
-        loads = ctx.enter_context(tc.tile_pool(name="loads", bufs=LOAD_AHEAD + 3))
-        feat_major = ctx.enter_context(tc.tile_pool(name="feat_major", bufs=4))
+        loads = ctx.enter_context(tc.tile_pool(name="loads", bufs=LOAD_AHEAD + 4))
+        feat_major = ctx.enter_context(tc.tile_pool(name="feat_major", bufs=5))
         v_pool = ctx.enter_context(tc.tile_pool(name="v_pool", bufs=5))
         work = ctx.enter_context(tc.tile_pool(name="work", bufs=3))
+        e_quant = ctx.enter_context(tc.tile_pool(name="e_quant", bufs=TILES_PER_WIN + 2))
         small = ctx.enter_context(tc.tile_pool(name="small", bufs=4))
         v_stage = ctx.enter_context(tc.tile_pool(name="v_stage", bufs=1))
         s_psum = ctx.enter_context(tc.psum_pool(name="s_psum", bufs=5))
         t_psum = ctx.enter_context(tc.psum_pool(name="t_psum", bufs=2))
-        o_psum = ctx.enter_context(tc.psum_pool(name="o_psum", bufs=1))
+        w_psum = ctx.enter_context(tc.psum_pool(name="w_psum", bufs=1))
         ctx.enter_context(tc.manual_schedule())
 
         ident_bf16 = consts.tile([P, P], BF16)
@@ -95,7 +96,7 @@ def tile_localattention_pa_kernel(tc, q, k, v, out):
             pad_logit[win] = pad_win
 
         def transpose_qk(win):
-            qk_ps = t_psum.tile([P, 2, TILES_PER_WIN, P], BF16, tag="transposed")
+            qk_ps = w_psum.tile([P, 2, TILES_PER_WIN, P], BF16, tag="window")
             for r in range(TILES_PER_WIN):
                 nc.tensor.transpose(qk_ps[:, 0, r, :], q_nat[win][:, r, :], ident_bf16[:])
                 u, h = divmod(r, 2)
@@ -213,8 +214,8 @@ def tile_localattention_pa_kernel(tc, q, k, v, out):
 
         def quantise_e(i):
             win = i // TILES_PER_WIN
-            codes = work.tile([P, 2 * P], U32, align_bytes=64)
-            scales = work.tile([P, 2 * P], U8, align_bytes=64)
+            codes = e_quant.tile([P, 2 * P], U32, align_bytes=64)
+            scales = e_quant.tile([P, 2 * P], U8, align_bytes=64)
             first = halves(win)[0] * P
             nc.vector.quantize_mx(
                 out=codes[:, first:].bitcast(FP8X4),
@@ -223,22 +224,22 @@ def tile_localattention_pa_kernel(tc, q, k, v, out):
             )
             e_codes[i], e_scales[i] = codes, scales
 
-        def weighted_v(i):
-            win, r = divmod(i, TILES_PER_WIN)
-            if r == 0:
-                o_ps = o_psum.tile([P, TILES_PER_WIN, FEAT], F32)
-                o_bank[win] = o_ps
-            for half in halves(win):
-                queries = slice(half * P, (half + 1) * P)
-                nc.tensor.matmul_mx(
-                    out=o_bank[win][:, r, :],
-                    lhsT=e_codes[i][:, queries].bitcast(FP8X4),
-                    lhsT_scale=e_scales[i][:, queries],
-                    rhs=v_codes[win - 1 + half][:].bitcast(FP8X4),
-                    rhs_scale=v_scales[win - 1 + half][:],
-                    start=(half == halves(win)[0]),
-                    stop=(half == CUR),
-                )
+        def weighted_v(win):
+            o_ps = w_psum.tile([P, TILES_PER_WIN, FEAT], F32, tag="window")
+            o_bank[win] = o_ps
+            for r in range(TILES_PER_WIN):
+                i = win * TILES_PER_WIN + r
+                for half in halves(win):
+                    queries = slice(half * P, (half + 1) * P)
+                    nc.tensor.matmul_mx(
+                        out=o_ps[:, r, :],
+                        lhsT=e_codes[i][:, queries].bitcast(FP8X4),
+                        lhsT_scale=e_scales[i][:, queries],
+                        rhs=v_codes[win - 1 + half][:].bitcast(FP8X4),
+                        rhs_scale=v_scales[win - 1 + half][:],
+                        start=(half == halves(win)[0]),
+                        stop=(half == CUR),
+                    )
 
         def sum_rows(win):
             total_win = small.tile([P, TILES_PER_WIN], F32)
@@ -293,7 +294,7 @@ def tile_localattention_pa_kernel(tc, q, k, v, out):
         for win in range(LOAD_AHEAD):
             load_window(win)
 
-        for n in range(-PREP_LEAD, TILES + 3):
+        for n in range(-PREP_LEAD, TILES + 4):
             prep_win = window_starting_at(n + PREP_LEAD)
             if prep_win is not None and prep_win + LOAD_AHEAD < WINDOWS:
                 load_window(prep_win + LOAD_AHEAD)
@@ -302,8 +303,10 @@ def tile_localattention_pa_kernel(tc, q, k, v, out):
                 scores(n + 2, BACK)
             if is_tile(n):
                 exponential(n, BACK)
-            if is_tile(n - 3):
-                weighted_v(n - 3)
+            if prep_win is not None:
+                transpose_qk(prep_win)
+            if window_starting_at(n - 6) is not None:
+                weighted_v(window_starting_at(n - 6))
             if is_tile(n + 2):
                 scores(n + 2, CUR)
             if is_tile(n):
@@ -328,11 +331,9 @@ def tile_localattention_pa_kernel(tc, q, k, v, out):
                 sum_rows(window_starting_at(n - 4))
             if window_starting_at(n - 5) is not None:
                 invert_sums(window_starting_at(n - 5))
-            if window_starting_at(n - 6) is not None:
-                finish(window_starting_at(n - 6))
-            if window_starting_at(n + 1) is not None:
-                quantise_v(window_starting_at(n + 1))
-            if window_starting_at(n + 5) is not None:
-                regroup_v(window_starting_at(n + 5))
-            if prep_win is not None:
-                transpose_qk(prep_win)
+            if window_starting_at(n - 7) is not None:
+                finish(window_starting_at(n - 7))
+            if window_starting_at(n) is not None:
+                quantise_v(window_starting_at(n))
+            if window_starting_at(n + 4) is not None:
+                regroup_v(window_starting_at(n + 4))

@@ -42,7 +42,7 @@ def tile_localattention_pa_kernel(tc, q, k, v, out):
         loads = ctx.enter_context(tc.tile_pool(name="loads", bufs=LOAD_AHEAD + 4))
         feat_major = ctx.enter_context(tc.tile_pool(name="feat_major", bufs=5))
         v_pool = ctx.enter_context(tc.tile_pool(name="v_pool", bufs=5))
-        work = ctx.enter_context(tc.tile_pool(name="work", bufs=3))
+        work = ctx.enter_context(tc.tile_pool(name="work", bufs=4))
         e_quant = ctx.enter_context(tc.tile_pool(name="e_quant", bufs=TILES_PER_WIN + 2))
         small = ctx.enter_context(tc.tile_pool(name="small", bufs=4))
         v_stage = ctx.enter_context(tc.tile_pool(name="v_stage", bufs=1))
@@ -253,7 +253,9 @@ def tile_localattention_pa_kernel(tc, q, k, v, out):
                 )
                 pad_total[win] = pad_sum
             else:
-                nc.vector.tensor_reduce(out=total_win[:], in_=row_sums[win][:], axis=AXIS.X, op=ALU.add)
+                nc.gpsimd.tensor_tensor(
+                    out=total_win[:], in0=row_sums[win][:, :, BACK], in1=row_sums[win][:, :, CUR], op=ALU.add
+                )
             total[win] = total_win
 
         def invert_sums(win):
@@ -294,7 +296,7 @@ def tile_localattention_pa_kernel(tc, q, k, v, out):
         for win in range(LOAD_AHEAD):
             load_window(win)
 
-        for n in range(-PREP_LEAD, TILES + 4):
+        for n in range(-PREP_LEAD, TILES + 5):
             prep_win = window_starting_at(n + PREP_LEAD)
             if prep_win is not None and prep_win + LOAD_AHEAD < WINDOWS:
                 load_window(prep_win + LOAD_AHEAD)
@@ -303,10 +305,10 @@ def tile_localattention_pa_kernel(tc, q, k, v, out):
                 scores(n + 2, BACK)
             if is_tile(n):
                 exponential(n, BACK)
-            if prep_win is not None:
-                transpose_qk(prep_win)
-            if window_starting_at(n - 6) is not None:
-                weighted_v(window_starting_at(n - 6))
+            if window_starting_at(n + PREP_LEAD - 1) is not None:
+                transpose_qk(window_starting_at(n + PREP_LEAD - 1))
+            if window_starting_at(n - 7) is not None:
+                weighted_v(window_starting_at(n - 7))
             if is_tile(n + 2):
                 scores(n + 2, CUR)
             if is_tile(n):
@@ -318,21 +320,21 @@ def tile_localattention_pa_kernel(tc, q, k, v, out):
 
             if is_tile(n + 1):
                 row_max(n + 1)
-            if is_tile(n - 2):
-                quantise_e(n - 2)
+            if is_tile(n - 3):
+                quantise_e(n - 3)
             if is_tile(n + 1):
                 exp_bias(n + 1)
 
             if prep_win is not None and has_padding(prep_win):
                 padding_logit(prep_win)
-            if window_starting_at(n + PREP_LEAD - 1) is not None:
-                copy_qk(window_starting_at(n + PREP_LEAD - 1))
-            if window_starting_at(n - 4) is not None:
-                sum_rows(window_starting_at(n - 4))
+            if window_starting_at(n + PREP_LEAD - 2) is not None:
+                copy_qk(window_starting_at(n + PREP_LEAD - 2))
             if window_starting_at(n - 5) is not None:
-                invert_sums(window_starting_at(n - 5))
-            if window_starting_at(n - 7) is not None:
-                finish(window_starting_at(n - 7))
+                sum_rows(window_starting_at(n - 5))
+            if window_starting_at(n - 6) is not None:
+                invert_sums(window_starting_at(n - 6))
+            if window_starting_at(n - 8) is not None:
+                finish(window_starting_at(n - 8))
             if window_starting_at(n) is not None:
                 quantise_v(window_starting_at(n))
             if window_starting_at(n + 4) is not None:

@@ -24,10 +24,12 @@ SCALE = FEAT**-0.5
 REAL_SCORES = WINDOWS * WIN * 2 * WIN - BATCH * WIN * WIN
 FLOPS = 2 * 2 * FEAT * REAL_SCORES
 
+Q, K = 0, 1
 BACK, CUR = 0, 1
 
-PREP_LEAD = 8
-LOAD_AHEAD = 3
+PREP_LEAD = 7
+LOAD_LEAD = 20
+FIRST_LOADS = 5
 
 
 def tile_localattention_pa_kernel(tc, q, k, v, out):
@@ -39,7 +41,7 @@ def tile_localattention_pa_kernel(tc, q, k, v, out):
 
     with ExitStack() as ctx:
         consts = ctx.enter_context(tc.tile_pool(name="consts", bufs=1))
-        loads = ctx.enter_context(tc.tile_pool(name="loads", bufs=LOAD_AHEAD + 4))
+        loads = ctx.enter_context(tc.tile_pool(name="loads", bufs=7))
         feat_major = ctx.enter_context(tc.tile_pool(name="feat_major", bufs=5))
         v_pool = ctx.enter_context(tc.tile_pool(name="v_pool", bufs=5))
         work = ctx.enter_context(tc.tile_pool(name="work", bufs=4))
@@ -72,13 +74,13 @@ def tile_localattention_pa_kernel(tc, q, k, v, out):
 
         def load_window(win):
             rows = slice(win * WIN, (win + 1) * WIN)
-            q_win = loads.tile([P, TILES_PER_WIN, FEAT], BF16)
-            nc.sync.dma_start(
-                out=q_win[:], in_=q_rows[rows, :].rearrange("(p r) d -> p r d", r=TILES_PER_WIN)
-            )
             k_win = loads.tile([P, 2, 2, FEAT], BF16)
             nc.sync.dma_start(
                 out=k_win[:], in_=k_rows[rows, :].rearrange("(h y u) d -> y h u d", h=2, u=2)
+            )
+            q_win = loads.tile([P, TILES_PER_WIN, FEAT], BF16)
+            nc.sync.dma_start(
+                out=q_win[:], in_=q_rows[rows, :].rearrange("(p r) d -> p r d", r=TILES_PER_WIN)
             )
             v_win = loads.tile([P, 2, 2, FEAT], BF16)
             nc.sync.dma_start(
@@ -95,17 +97,40 @@ def tile_localattention_pa_kernel(tc, q, k, v, out):
             )
             pad_logit[win] = pad_win
 
+        def transpose_q(win, bank):
+            for r in range(TILES_PER_WIN):
+                nc.tensor.transpose(bank[:, Q, r, :], q_nat[win][:, r, :], ident_bf16[:])
+
+        def transpose_k(win, bank):
+            for r in range(TILES_PER_WIN):
+                u, h = divmod(r, 2)
+                nc.tensor.transpose(bank[:, K, r, :], k_nat[win][:, h, u, :], ident_bf16[:])
+
+        def prepare_first_window():
+            k_ps = w_psum.tile([P, 2, TILES_PER_WIN, P], BF16, tag="window")
+            transpose_k(0, k_ps)
+            q_ps = t_psum.tile([P, 2, TILES_PER_WIN, P], BF16, tag="transposed")
+            transpose_q(0, q_ps)
+            qk_win = feat_major.tile([P, 2, TILES_PER_WIN, P], BF16)
+            nc.vector.tensor_copy(out=qk_win[:, K, :, :], in_=k_ps[:, K, :, :])
+            nc.scalar.copy(out=qk_win[:, Q, :, :], in_=q_ps[:, Q, :, :])
+            qk_t[0] = qk_win
+
         def transpose_qk(win):
             qk_ps = w_psum.tile([P, 2, TILES_PER_WIN, P], BF16, tag="window")
-            for r in range(TILES_PER_WIN):
-                nc.tensor.transpose(qk_ps[:, 0, r, :], q_nat[win][:, r, :], ident_bf16[:])
-                u, h = divmod(r, 2)
-                nc.tensor.transpose(qk_ps[:, 1, r, :], k_nat[win][:, h, u, :], ident_bf16[:])
+            transpose_q(win, qk_ps)
+            transpose_k(win, qk_ps)
             qk_bank[win] = qk_ps
+
+        def copied_by_scalar(win):
+            return win == 1 or has_padding(win - 2)
 
         def copy_qk(win):
             qk_win = feat_major.tile([P, 2, TILES_PER_WIN, P], BF16)
-            nc.vector.tensor_copy(out=qk_win[:], in_=qk_bank[win][:])
+            if copied_by_scalar(win):
+                nc.scalar.copy(out=qk_win[:], in_=qk_bank[win][:])
+            else:
+                nc.vector.tensor_copy(out=qk_win[:], in_=qk_bank[win][:])
             qk_t[win] = qk_win
 
         def regroup_v(win):
@@ -134,11 +159,11 @@ def tile_localattention_pa_kernel(tc, q, k, v, out):
             win, r = divmod(i, TILES_PER_WIN)
             if half not in halves(win):
                 return
-            s_ps = s_psum.tile([P, WIN], F32)
+            s_ps = s_psum.tile([P, WIN], F32, tag="scores")
             nc.tensor.matmul(
                 out=s_ps[:],
-                lhsT=qk_t[win][:, 0, r, :],
-                rhs=qk_t[win - 1 + half][:, 1, :, :].rearrange("d j p -> d (j p)"),
+                lhsT=qk_t[win][:, Q, r, :],
+                rhs=qk_t[win - 1 + half][:, K, :, :].rearrange("d j p -> d (j p)"),
                 start=True,
                 stop=True,
             )
@@ -157,7 +182,8 @@ def tile_localattention_pa_kernel(tc, q, k, v, out):
             win, r = divmod(i, TILES_PER_WIN)
             other = pad_logit[win][:, r : r + 1] if has_padding(win) else row_top[i][:, BACK : BACK + 1]
             bias_i = small.tile([P, 1], F32)
-            nc.gpsimd.tensor_scalar(
+            engine = nc.vector if i == 0 else nc.gpsimd
+            engine.tensor_scalar(
                 out=bias_i[:],
                 in0=row_top[i][:, CUR : CUR + 1],
                 scalar1=other,
@@ -229,10 +255,15 @@ def tile_localattention_pa_kernel(tc, q, k, v, out):
             o_bank[win] = o_ps
             for r in range(TILES_PER_WIN):
                 i = win * TILES_PER_WIN + r
+                out_i = o_ps[:, r, :]
+                if i == TILES - 1:
+                    o_last = s_psum.tile([P, WIN], F32, tag="scores")
+                    o_bank[WINDOWS] = o_last
+                    out_i = o_last[:, :FEAT]
                 for half in halves(win):
                     queries = slice(half * P, (half + 1) * P)
                     nc.tensor.matmul_mx(
-                        out=o_ps[:, r, :],
+                        out=out_i,
                         lhsT=e_codes[i][:, queries].bitcast(FP8X4),
                         lhsT_scale=e_scales[i][:, queries],
                         rhs=v_codes[win - 1 + half][:].bitcast(FP8X4),
@@ -276,16 +307,28 @@ def tile_localattention_pa_kernel(tc, q, k, v, out):
                         op1=ALU.mult,
                     )
             else:
+                tiles = TILES_PER_WIN - 1 if win == WINDOWS - 1 else TILES_PER_WIN
                 nc.vector.tensor_tensor(
-                    out=o_sb[:],
-                    in0=o_bank[win][:],
-                    in1=inverse[win][:].unsqueeze(2).to_broadcast([P, TILES_PER_WIN, FEAT]),
+                    out=o_sb[:, :tiles, :],
+                    in0=o_bank[win][:, :tiles, :],
+                    in1=inverse[win][:, :tiles].unsqueeze(2).to_broadcast([P, tiles, FEAT]),
                     op=ALU.mult,
                 )
             rows = slice(win * WIN, (win + 1) * WIN)
-            nc.sync.dma_start(
-                out=out_rows[rows, :].rearrange("(p r) d -> p r d", r=TILES_PER_WIN), in_=o_sb[:]
-            )
+            dst = out_rows[rows, :].rearrange("(p r) d -> p r d", r=TILES_PER_WIN)
+            if win < WINDOWS - 1:
+                nc.sync.dma_start(out=dst, in_=o_sb[:])
+            else:
+                last = TILES_PER_WIN - 1
+                nc.sync.dma_start(out=dst[:, :last, :], in_=o_sb[:, :last, :])
+                nc.vector.tensor_scalar(
+                    out=o_sb[:, last, :],
+                    in0=o_bank[WINDOWS][:, :FEAT],
+                    scalar1=inverse[win][:, last:],
+                    scalar2=None,
+                    op0=ALU.mult,
+                )
+                nc.sync.dma_start(out=dst[:, last:, :], in_=o_sb[:, last:, :])
 
         def is_tile(i):
             return 0 <= i < TILES
@@ -293,30 +336,42 @@ def tile_localattention_pa_kernel(tc, q, k, v, out):
         def window_starting_at(i):
             return i // TILES_PER_WIN if is_tile(i) and i % TILES_PER_WIN == 0 else None
 
-        for win in range(LOAD_AHEAD):
-            load_window(win)
+        def preparing(n):
+            if n == -1:
+                return 1
+            return window_starting_at(n + PREP_LEAD) if n > 0 else None
 
-        for n in range(-PREP_LEAD, TILES + 5):
-            prep_win = window_starting_at(n + PREP_LEAD)
-            if prep_win is not None and prep_win + LOAD_AHEAD < WINDOWS:
-                load_window(prep_win + LOAD_AHEAD)
+        for win in range(FIRST_LOADS):
+            load_window(win)
+        regroup_v(0)
+        prepare_first_window()
+        padding_logit(0)
+
+        for n in range(-2, TILES + 5):
+            if window_starting_at(n + LOAD_LEAD) is not None:
+                load_window(window_starting_at(n + LOAD_LEAD))
 
             if is_tile(n + 2):
                 scores(n + 2, BACK)
             if is_tile(n):
                 exponential(n, BACK)
-            if window_starting_at(n + PREP_LEAD - 1) is not None:
-                transpose_qk(window_starting_at(n + PREP_LEAD - 1))
+            if preparing(n) is not None and n > 0:
+                transpose_qk(preparing(n))
             if window_starting_at(n - 7) is not None:
                 weighted_v(window_starting_at(n - 7))
             if is_tile(n + 2):
                 scores(n + 2, CUR)
+            if n == -1:
+                transpose_qk(preparing(n))
             if is_tile(n):
                 exponential(n, CUR)
             if is_tile(n - 1):
                 regroup_e(n - 1)
             if is_tile(n):
                 transpose_e(n)
+            copying = preparing(n - 1)
+            if copying is not None and copied_by_scalar(copying):
+                copy_qk(copying)
 
             if is_tile(n + 1):
                 row_max(n + 1)
@@ -325,10 +380,11 @@ def tile_localattention_pa_kernel(tc, q, k, v, out):
             if is_tile(n + 1):
                 exp_bias(n + 1)
 
-            if prep_win is not None and has_padding(prep_win):
-                padding_logit(prep_win)
-            if window_starting_at(n + PREP_LEAD - 2) is not None:
-                copy_qk(window_starting_at(n + PREP_LEAD - 2))
+            soon = window_starting_at(n + PREP_LEAD + 1)
+            if soon is not None and has_padding(soon):
+                padding_logit(soon)
+            if copying is not None and not copied_by_scalar(copying):
+                copy_qk(copying)
             if window_starting_at(n - 5) is not None:
                 sum_rows(window_starting_at(n - 5))
             if window_starting_at(n - 6) is not None:
@@ -337,5 +393,5 @@ def tile_localattention_pa_kernel(tc, q, k, v, out):
                 finish(window_starting_at(n - 8))
             if window_starting_at(n) is not None:
                 quantise_v(window_starting_at(n))
-            if window_starting_at(n + 4) is not None:
+            if n >= 0 and window_starting_at(n + 4) is not None:
                 regroup_v(window_starting_at(n + 4))

@@ -19,6 +19,7 @@ WINDOWS_PER_SEQ = SEQ // WIN
 WINDOWS = BATCH * WINDOWS_PER_SEQ
 TILES_PER_WIN = WIN // P
 TILES = WINDOWS * TILES_PER_WIN
+PAIR = 2
 SCALE = FEAT**-0.5
 
 REAL_SCORES = WINDOWS * WIN * 2 * WIN - BATCH * WIN * WIN
@@ -45,7 +46,7 @@ def tile_localattention_pa_kernel(tc, q, k, v, out):
         feat_major = ctx.enter_context(tc.tile_pool(name="feat_major", bufs=5))
         v_pool = ctx.enter_context(tc.tile_pool(name="v_pool", bufs=5))
         work = ctx.enter_context(tc.tile_pool(name="work", bufs=4))
-        e_quant = ctx.enter_context(tc.tile_pool(name="e_quant", bufs=TILES_PER_WIN + 2))
+        e_quant = ctx.enter_context(tc.tile_pool(name="e_quant", bufs=4))
         small = ctx.enter_context(tc.tile_pool(name="small", bufs=4))
         v_stage = ctx.enter_context(tc.tile_pool(name="v_stage", bufs=1))
         s_psum = ctx.enter_context(tc.psum_pool(name="s_psum", bufs=5))
@@ -231,24 +232,26 @@ def tile_localattention_pa_kernel(tc, q, k, v, out):
 
         def regroup_e(i):
             win = i // TILES_PER_WIN
-            grouped = work.tile([P, 2 * P * PACK], BF16, align_bytes=64)
-            dst = grouped[:].bitcast(F32).rearrange("p (h m u) -> p h m u", h=2, u=2)
+            pair, j = divmod(i, PAIR)
+            if j == 0:
+                grouped = work.tile([P, 2 * PAIR * P * PACK], BF16, align_bytes=64)
+                e_grouped[pair] = grouped
+            dst = e_grouped[pair][:].bitcast(F32).rearrange("p (h j m u) -> p h j m u", h=2, j=PAIR, u=2)
             src = t_bank[i][:].rearrange("p h u m -> p h m u")
             first = halves(win)[0]
-            nc.scalar.copy(out=dst[:, first:, :, :], in_=src[:, first:, :, :])
-            e_grouped[i] = grouped
+            nc.scalar.copy(out=dst[:, first:, j, :, :], in_=src[:, first:, :, :])
 
-        def quantise_e(i):
-            win = i // TILES_PER_WIN
-            codes = e_quant.tile([P, 2 * P], U32, align_bytes=64)
-            scales = e_quant.tile([P, 2 * P], U8, align_bytes=64)
-            first = halves(win)[0] * P
+        def quantise_e(pair):
+            win = pair * PAIR // TILES_PER_WIN
+            codes = e_quant.tile([P, 2 * PAIR * P], U32, align_bytes=64)
+            scales = e_quant.tile([P, 2 * PAIR * P], U8, align_bytes=64)
+            first = halves(win)[0] * PAIR * P
             nc.vector.quantize_mx(
                 out=codes[:, first:].bitcast(FP8X4),
                 scales=scales[:, first:],
-                in_=e_grouped[i][:, first * PACK :],
+                in_=e_grouped[pair][:, first * PACK :],
             )
-            e_codes[i], e_scales[i] = codes, scales
+            e_codes[pair], e_scales[pair] = codes, scales
 
         def weighted_v(win):
             o_ps = w_psum.tile([P, TILES_PER_WIN, FEAT], F32, tag="window")
@@ -260,12 +263,14 @@ def tile_localattention_pa_kernel(tc, q, k, v, out):
                     o_last = s_psum.tile([P, WIN], F32, tag="scores")
                     o_bank[WINDOWS] = o_last
                     out_i = o_last[:, :FEAT]
+                pair, j = divmod(i, PAIR)
                 for half in halves(win):
-                    queries = slice(half * P, (half + 1) * P)
+                    first = (half * PAIR + j) * P
+                    queries = slice(first, first + P)
                     nc.tensor.matmul_mx(
                         out=out_i,
-                        lhsT=e_codes[i][:, queries].bitcast(FP8X4),
-                        lhsT_scale=e_scales[i][:, queries],
+                        lhsT=e_codes[pair][:, queries].bitcast(FP8X4),
+                        lhsT_scale=e_scales[pair][:, queries],
                         rhs=v_codes[win - 1 + half][:].bitcast(FP8X4),
                         rhs_scale=v_scales[win - 1 + half][:],
                         start=(half == halves(win)[0]),
@@ -375,8 +380,8 @@ def tile_localattention_pa_kernel(tc, q, k, v, out):
 
             if is_tile(n + 1):
                 row_max(n + 1)
-            if is_tile(n - 3):
-                quantise_e(n - 3)
+            if n % 2 == 1 and is_tile(n - 3):
+                quantise_e((n - 3) // PAIR)
             if is_tile(n + 1):
                 exp_bias(n + 1)
 

@@ -225,32 +225,35 @@ def tile_localattention_pa_kernel(tc, q, k, v, out):
             t_ps = t_psum.tile([P, 2, 2, P], F32, tag="transposed")
             e_words = e_rows[i][:].bitcast(F32)
             for half in halves(win):
+                if i == TILES - 1 and half == CUR:
+                    t_ps = s_psum.tile([P, 2, 2, P], F32, tag="scores")
                 for u in range(2):
                     first = (2 * half + u) * P
                     nc.tensor.transpose(t_ps[:, half, u, :], e_words[:, first : first + P], ident_f32[:])
-            t_bank[i] = t_ps
+                t_bank[i, half] = t_ps
 
-        def regroup_e(i):
-            win = i // TILES_PER_WIN
+        def regroup_e(i, first, last, copy):
             pair, j = divmod(i, PAIR)
-            if j == 0:
+            if pair not in e_grouped:
                 grouped = work.tile([P, 2 * PAIR * P * PACK], BF16, align_bytes=64)
                 e_grouped[pair] = grouped
             dst = e_grouped[pair][:].bitcast(F32).rearrange("p (h j m u) -> p h j m u", h=2, j=PAIR, u=2)
-            src = t_bank[i][:].rearrange("p h u m -> p h m u")
-            first = halves(win)[0]
-            nc.scalar.copy(out=dst[:, first:, j, :, :], in_=src[:, first:, :, :])
+            src = t_bank[i, last][:].rearrange("p h u m -> p h m u")
+            copy(out=dst[:, first : last + 1, j, :, :], in_=src[:, first : last + 1, :, :])
 
         def quantise_e(pair):
             win = pair * PAIR // TILES_PER_WIN
             codes = e_quant.tile([P, 2 * PAIR * P], U32, align_bytes=64)
             scales = e_quant.tile([P, 2 * PAIR * P], U8, align_bytes=64)
-            first = halves(win)[0] * PAIR * P
-            nc.vector.quantize_mx(
-                out=codes[:, first:].bitcast(FP8X4),
-                scales=scales[:, first:],
-                in_=e_grouped[pair][:, first * PACK :],
-            )
+            parts = [(halves(win)[0] * PAIR * P, 2 * PAIR * P)]
+            if pair == TILES // PAIR - 1:
+                parts = [((half * PAIR + j) * P, (half * PAIR + j + 1) * P) for j in range(PAIR) for half in range(2)]
+            for first, end in parts:
+                nc.vector.quantize_mx(
+                    out=codes[:, first:end].bitcast(FP8X4),
+                    scales=scales[:, first:end],
+                    in_=e_grouped[pair][:, first * PACK : end * PACK],
+                )
             e_codes[pair], e_scales[pair] = codes, scales
 
         def weighted_v(win):
@@ -370,8 +373,10 @@ def tile_localattention_pa_kernel(tc, q, k, v, out):
                 transpose_qk(preparing(n))
             if is_tile(n):
                 exponential(n, CUR)
-            if is_tile(n - 1):
-                regroup_e(n - 1)
+            if n == TILES:
+                regroup_e(n - 1, CUR, CUR, nc.scalar.copy)
+            elif is_tile(n - 1):
+                regroup_e(n - 1, halves((n - 1) // TILES_PER_WIN)[0], CUR, nc.scalar.copy)
             if is_tile(n):
                 transpose_e(n)
             copying = preparing(n - 1)
@@ -382,6 +387,8 @@ def tile_localattention_pa_kernel(tc, q, k, v, out):
                 row_max(n + 1)
             if n % 2 == 1 and is_tile(n - 3):
                 quantise_e((n - 3) // PAIR)
+            if window_starting_at(n - 3) is not None:
+                quantise_v(window_starting_at(n - 3))
             if is_tile(n + 1):
                 exp_bias(n + 1)
 
@@ -396,7 +403,7 @@ def tile_localattention_pa_kernel(tc, q, k, v, out):
                 invert_sums(window_starting_at(n - 6))
             if window_starting_at(n - 8) is not None:
                 finish(window_starting_at(n - 8))
-            if window_starting_at(n) is not None:
-                quantise_v(window_starting_at(n))
-            if n >= 0 and window_starting_at(n + 4) is not None:
-                regroup_v(window_starting_at(n + 4))
+            if n == TILES:
+                regroup_e(n - 1, BACK, BACK, nc.vector.tensor_copy)
+            if n > 0 and window_starting_at(n + 1) is not None:
+                regroup_v(window_starting_at(n + 1))

@@ -98,8 +98,8 @@ def tile_localattention_pa_kernel(tc, q, k, v, out):
             )
             pad_logit[win] = pad_win
 
-        def transpose_q(win, bank):
-            for r in range(TILES_PER_WIN):
+        def transpose_q(win, bank, tiles=range(TILES_PER_WIN)):
+            for r in tiles:
                 nc.tensor.transpose(bank[:, Q, r, :], q_nat[win][:, r, :], ident_bf16[:])
 
         def transpose_k(win, bank):
@@ -110,11 +110,13 @@ def tile_localattention_pa_kernel(tc, q, k, v, out):
         def prepare_first_window():
             k_ps = w_psum.tile([P, 2, TILES_PER_WIN, P], BF16, tag="window")
             transpose_k(0, k_ps)
-            q_ps = t_psum.tile([P, 2, TILES_PER_WIN, P], BF16, tag="transposed")
-            transpose_q(0, q_ps)
             qk_win = feat_major.tile([P, 2, TILES_PER_WIN, P], BF16)
             nc.vector.tensor_copy(out=qk_win[:, K, :, :], in_=k_ps[:, K, :, :])
-            nc.scalar.copy(out=qk_win[:, Q, :, :], in_=q_ps[:, Q, :, :])
+            for tiles in (range(1), range(1, TILES_PER_WIN)):
+                q_ps = t_psum.tile([P, 2, TILES_PER_WIN, P], BF16, tag="transposed")
+                transpose_q(0, q_ps, tiles)
+                part = slice(tiles.start, tiles.stop)
+                nc.scalar.copy(out=qk_win[:, Q, part, :], in_=q_ps[:, Q, part, :])
             qk_t[0] = qk_win
 
         def transpose_qk(win):
@@ -183,7 +185,7 @@ def tile_localattention_pa_kernel(tc, q, k, v, out):
             win, r = divmod(i, TILES_PER_WIN)
             other = pad_logit[win][:, r : r + 1] if has_padding(win) else row_top[i][:, BACK : BACK + 1]
             bias_i = small.tile([P, 1], F32)
-            engine = nc.vector if i == 0 else nc.gpsimd
+            engine = nc.vector if i % 2 == 0 else nc.gpsimd
             engine.tensor_scalar(
                 out=bias_i[:],
                 in0=row_top[i][:, CUR : CUR + 1],

@@ -185,7 +185,7 @@ def tile_localattention_pa_kernel(tc, q, k, v, out):
             win, r = divmod(i, TILES_PER_WIN)
             other = pad_logit[win][:, r : r + 1] if has_padding(win) else row_top[i][:, BACK : BACK + 1]
             bias_i = small.tile([P, 1], F32)
-            engine = nc.vector if i % 2 == 0 else nc.gpsimd
+            engine = nc.vector if i == 0 else nc.gpsimd
             engine.tensor_scalar(
                 out=bias_i[:],
                 in0=row_top[i][:, CUR : CUR + 1],
@@ -391,6 +391,8 @@ def tile_localattention_pa_kernel(tc, q, k, v, out):
                 quantise_e((n - 3) // PAIR)
             if window_starting_at(n - 3) is not None:
                 quantise_v(window_starting_at(n - 3))
+            if window_starting_at(n - 7) is not None:
+                invert_sums(window_starting_at(n - 7))
             if is_tile(n + 1):
                 exp_bias(n + 1)
 
@@ -401,8 +403,6 @@ def tile_localattention_pa_kernel(tc, q, k, v, out):
                 copy_qk(copying)
             if window_starting_at(n - 5) is not None:
                 sum_rows(window_starting_at(n - 5))
-            if window_starting_at(n - 6) is not None:
-                invert_sums(window_starting_at(n - 6))
             if window_starting_at(n - 8) is not None:
                 finish(window_starting_at(n - 8))
             if n == TILES:

from contextlib import ExitStack

import concourse.mybir as mybir
from concourse.masks import make_identity

BF16 = mybir.dt.bfloat16
F32 = mybir.dt.float32
U32 = mybir.dt.uint32
U8 = mybir.dt.uint8
FP8X4 = mybir.dt.float8_e4m3fn_x4
ACT = mybir.ActivationFunctionType
ALU = mybir.AluOpType
AXIS = mybir.AxisListType

BATCH, SEQ, FEAT, WIN = 2, 8192, 128, 512
P = 128
PACK = 4
WINDOWS_PER_SEQ = SEQ // WIN
WINDOWS = BATCH * WINDOWS_PER_SEQ
TILES_PER_WIN = WIN // P
TILES = WINDOWS * TILES_PER_WIN
PAIR = 2
SCALE = FEAT**-0.5

REAL_SCORES = WINDOWS * WIN * 2 * WIN - BATCH * WIN * WIN
FLOPS = 2 * 2 * FEAT * REAL_SCORES

Q, K = 0, 1
BACK, CUR = 0, 1

PREP_LEAD = 7
LOAD_LEAD = 20
FIRST_LOADS = 5


def tile_localattention_pa_kernel(tc, q, k, v, out):
    nc = tc.nc
    q_rows = q.flatten_outer_dims()
    k_rows = k.flatten_outer_dims()
    v_rows = v.flatten_outer_dims()
    out_rows = out.flatten_outer_dims()

    with ExitStack() as ctx:
        consts = ctx.enter_context(tc.tile_pool(name="consts", bufs=1))
        loads = ctx.enter_context(tc.tile_pool(name="loads", bufs=7))
        feat_major = ctx.enter_context(tc.tile_pool(name="feat_major", bufs=5))
        v_pool = ctx.enter_context(tc.tile_pool(name="v_pool", bufs=5))
        work = ctx.enter_context(tc.tile_pool(name="work", bufs=4))
        e_quant = ctx.enter_context(tc.tile_pool(name="e_quant", bufs=4))
        small = ctx.enter_context(tc.tile_pool(name="small", bufs=4))
        v_stage = ctx.enter_context(tc.tile_pool(name="v_stage", bufs=1))
        s_psum = ctx.enter_context(tc.psum_pool(name="s_psum", bufs=5))
        t_psum = ctx.enter_context(tc.psum_pool(name="t_psum", bufs=2))
        w_psum = ctx.enter_context(tc.psum_pool(name="w_psum", bufs=1))
        ctx.enter_context(tc.manual_schedule())

        ident_bf16 = consts.tile([P, P], BF16)
        make_identity(nc, ident_bf16[:])
        ident_f32 = consts.tile([P, P], F32)
        make_identity(nc, ident_f32[:])

        q_nat, k_nat, v_nat = {}, {}, {}
        qk_bank, qk_t = {}, {}
        v_grouped, v_codes, v_scales = {}, {}, {}
        pad_logit = {}
        s_bank, row_top, bias, e_rows, row_sums = {}, {}, {}, {}, {}
        t_bank, e_grouped, e_codes, e_scales = {}, {}, {}, {}
        o_bank, pad_total, total, inverse = {}, {}, {}, {}

        def has_padding(win):
            return win % WINDOWS_PER_SEQ == 0

        def halves(win):
            return (CUR,) if has_padding(win) else (BACK, CUR)

        def load_window(win):
            rows = slice(win * WIN, (win + 1) * WIN)
            k_win = loads.tile([P, 2, 2, FEAT], BF16)
            nc.sync.dma_start(
                out=k_win[:], in_=k_rows[rows, :].rearrange("(h y u) d -> y h u d", h=2, u=2)
            )
            q_win = loads.tile([P, TILES_PER_WIN, FEAT], BF16)
            nc.sync.dma_start(
                out=q_win[:], in_=q_rows[rows, :].rearrange("(p r) d -> p r d", r=TILES_PER_WIN)
            )
            v_win = loads.tile([P, 2, 2, FEAT], BF16)
            nc.sync.dma_start(
                out=v_win[:], in_=v_rows[rows, :].rearrange("(p c u) d -> p c u d", c=2, u=2)
            )
            q_nat[win], k_nat[win], v_nat[win] = q_win, k_win, v_win

        def padding_logit(win):
            q_sum = small.tile([P, TILES_PER_WIN], F32)
            nc.vector.tensor_reduce(out=q_sum[:], in_=q_nat[win][:], axis=AXIS.X, op=ALU.add)
            pad_win = small.tile([P, TILES_PER_WIN], F32)
            nc.vector.tensor_scalar(
                out=pad_win[:], in0=q_sum[:], scalar1=-1.0, scalar2=None, op0=ALU.mult
            )
            pad_logit[win] = pad_win

        def transpose_q(win, bank, tiles=range(TILES_PER_WIN)):
            for r in tiles:
                nc.tensor.transpose(bank[:, Q, r, :], q_nat[win][:, r, :], ident_bf16[:])

        def transpose_k(win, bank):
            for r in range(TILES_PER_WIN):
                u, h = divmod(r, 2)
                nc.tensor.transpose(bank[:, K, r, :], k_nat[win][:, h, u, :], ident_bf16[:])

        def prepare_first_window():
            k_ps = w_psum.tile([P, 2, TILES_PER_WIN, P], BF16, tag="window")
            transpose_k(0, k_ps)
            qk_win = feat_major.tile([P, 2, TILES_PER_WIN, P], BF16)
            nc.vector.tensor_copy(out=qk_win[:, K, :, :], in_=k_ps[:, K, :, :])
            for tiles in (range(1), range(1, TILES_PER_WIN)):
                q_ps = t_psum.tile([P, 2, TILES_PER_WIN, P], BF16, tag="transposed")
                transpose_q(0, q_ps, tiles)
                part = slice(tiles.start, tiles.stop)
                nc.scalar.copy(out=qk_win[:, Q, part, :], in_=q_ps[:, Q, part, :])
            qk_t[0] = qk_win

        def transpose_qk(win):
            qk_ps = w_psum.tile([P, 2, TILES_PER_WIN, P], BF16, tag="window")
            transpose_q(win, qk_ps)
            transpose_k(win, qk_ps)
            qk_bank[win] = qk_ps

        def copied_by_scalar(win):
            return win == 1 or has_padding(win - 2)

        def copy_qk(win):
            qk_win = feat_major.tile([P, 2, TILES_PER_WIN, P], BF16)
            if copied_by_scalar(win):
                nc.scalar.copy(out=qk_win[:], in_=qk_bank[win][:])
            else:
                nc.vector.tensor_copy(out=qk_win[:], in_=qk_bank[win][:])
            qk_t[win] = qk_win

        def regroup_v(win):
            v_group_win = v_stage.tile([P, FEAT, 2, 2], BF16, align_bytes=64)
            nc.gpsimd.tensor_scalar(
                out=v_group_win[:],
                in0=v_nat[win][:].rearrange("p c u d -> p d u c"),
                scalar1=1.0,
                scalar2=0.0,
                op0=ALU.mult,
                op1=ALU.add,
            )
            v_grouped[win] = v_group_win

        def quantise_v(win):
            v_code_win = v_pool.tile([P, FEAT], U32, align_bytes=64)
            v_scale_win = v_pool.tile([P, FEAT], U8, align_bytes=64)
            nc.vector.quantize_mx(
                out=v_code_win[:].bitcast(FP8X4),
                scales=v_scale_win[:],
                in_=v_grouped[win][:].rearrange("p d u c -> p (d u c)"),
            )
            v_codes[win], v_scales[win] = v_code_win, v_scale_win

        def scores(i, half):
            win, r = divmod(i, TILES_PER_WIN)
            if half not in halves(win):
                return
            s_ps = s_psum.tile([P, WIN], F32, tag="scores")
            nc.tensor.matmul(
                out=s_ps[:],
                lhsT=qk_t[win][:, Q, r, :],
                rhs=qk_t[win - 1 + half][:, K, :, :].rearrange("d j p -> d (j p)"),
                start=True,
                stop=True,
            )
            s_bank[i, half] = s_ps

        def row_max(i):
            win, r = divmod(i, TILES_PER_WIN)
            top = small.tile([P, 2], F32)
            for half in halves(win):
                nc.vector.tensor_reduce(
                    out=top[:, half : half + 1], in_=s_bank[i, half][:], axis=AXIS.X, op=ALU.max
                )
            row_top[i] = top

        def exp_bias(i):
            win, r = divmod(i, TILES_PER_WIN)
            other = pad_logit[win][:, r : r + 1] if has_padding(win) else row_top[i][:, BACK : BACK + 1]
            bias_i = small.tile([P, 1], F32)
            engine = nc.vector if i == 0 else nc.gpsimd
            engine.tensor_scalar(
                out=bias_i[:],
                in0=row_top[i][:, CUR : CUR + 1],
                scalar1=other,
                scalar2=-SCALE,
                op0=ALU.max,
                op1=ALU.mult,
            )
            bias[i] = bias_i

        def exponential(i, half):
            win, r = divmod(i, TILES_PER_WIN)
            if half == BACK:
                e_tile = work.tile([P, 2 * WIN], BF16)
                e_rows[i] = e_tile
                if r == 0:
                    sums_win = small.tile([P, TILES_PER_WIN, 2], F32)
                    row_sums[win] = sums_win
            if half in halves(win):
                nc.scalar.activation(
                    out=e_rows[i][:, half * WIN : (half + 1) * WIN],
                    in_=s_bank[i, half][:],
                    func=ACT.Exp,
                    bias=bias[i][:],
                    scale=SCALE,
                    accum_out=row_sums[win][:, r, half : half + 1],
                )
            else:
                nc.scalar.activation(
                    out=row_sums[win][:, r, half : half + 1],
                    in_=pad_logit[win][:, r : r + 1],
                    func=ACT.Exp,
                    bias=bias[i][:],
                    scale=SCALE,
                )

        def transpose_e(i):
            win = i // TILES_PER_WIN
            t_ps = t_psum.tile([P, 2, 2, P], F32, tag="transposed")
            e_words = e_rows[i][:].bitcast(F32)
            for half in halves(win):
                if i == TILES - 1 and half == CUR:
                    t_ps = s_psum.tile([P, 2, 2, P], F32, tag="scores")
                for u in range(2):
                    first = (2 * half + u) * P
                    nc.tensor.transpose(t_ps[:, half, u, :], e_words[:, first : first + P], ident_f32[:])
                t_bank[i, half] = t_ps

        def regroup_e(i, first, last, copy):
            pair, j = divmod(i, PAIR)
            if pair not in e_grouped:
                grouped = work.tile([P, 2 * PAIR * P * PACK], BF16, align_bytes=64)
                e_grouped[pair] = grouped
            dst = e_grouped[pair][:].bitcast(F32).rearrange("p (h j m u) -> p h j m u", h=2, j=PAIR, u=2)
            src = t_bank[i, last][:].rearrange("p h u m -> p h m u")
            copy(out=dst[:, first : last + 1, j, :, :], in_=src[:, first : last + 1, :, :])

        def quantise_e(pair):
            win = pair * PAIR // TILES_PER_WIN
            codes = e_quant.tile([P, 2 * PAIR * P], U32, align_bytes=64)
            scales = e_quant.tile([P, 2 * PAIR * P], U8, align_bytes=64)
            parts = [(halves(win)[0] * PAIR * P, 2 * PAIR * P)]
            if pair == TILES // PAIR - 1:
                parts = [((half * PAIR + j) * P, (half * PAIR + j + 1) * P) for j in range(PAIR) for half in range(2)]
            for first, end in parts:
                nc.vector.quantize_mx(
                    out=codes[:, first:end].bitcast(FP8X4),
                    scales=scales[:, first:end],
                    in_=e_grouped[pair][:, first * PACK : end * PACK],
                )
            e_codes[pair], e_scales[pair] = codes, scales

        def weighted_v(win):
            o_ps = w_psum.tile([P, TILES_PER_WIN, FEAT], F32, tag="window")
            o_bank[win] = o_ps
            for r in range(TILES_PER_WIN):
                i = win * TILES_PER_WIN + r
                out_i = o_ps[:, r, :]
                if i == TILES - 1:
                    o_last = s_psum.tile([P, WIN], F32, tag="scores")
                    o_bank[WINDOWS] = o_last
                    out_i = o_last[:, :FEAT]
                pair, j = divmod(i, PAIR)
                for half in halves(win):
                    first = (half * PAIR + j) * P
                    queries = slice(first, first + P)
                    nc.tensor.matmul_mx(
                        out=out_i,
                        lhsT=e_codes[pair][:, queries].bitcast(FP8X4),
                        lhsT_scale=e_scales[pair][:, queries],
                        rhs=v_codes[win - 1 + half][:].bitcast(FP8X4),
                        rhs_scale=v_scales[win - 1 + half][:],
                        start=(half == halves(win)[0]),
                        stop=(half == CUR),
                    )

        def sum_rows(win):
            total_win = small.tile([P, TILES_PER_WIN], F32)
            if has_padding(win):
                pad_sum = small.tile([P, TILES_PER_WIN], F32)
                nc.vector.tensor_scalar(
                    out=pad_sum[:], in0=row_sums[win][:, :, BACK], scalar1=float(WIN), scalar2=None, op0=ALU.mult
                )
                nc.vector.tensor_tensor(
                    out=total_win[:], in0=pad_sum[:], in1=row_sums[win][:, :, CUR], op=ALU.add
                )
                pad_total[win] = pad_sum
            else:
                nc.gpsimd.tensor_tensor(
                    out=total_win[:], in0=row_sums[win][:, :, BACK], in1=row_sums[win][:, :, CUR], op=ALU.add
                )
            total[win] = total_win

        def invert_sums(win):
            inverse_win = small.tile([P, TILES_PER_WIN], F32)
            nc.vector.reciprocal(out=inverse_win[:], in_=total[win][:])
            inverse[win] = inverse_win

        def finish(win):
            o_sb = work.tile([P, TILES_PER_WIN, FEAT], F32)
            if has_padding(win):
                for r in range(TILES_PER_WIN):
                    nc.vector.tensor_scalar(
                        out=o_sb[:, r, :],
                        in0=o_bank[win][:, r, :],
                        scalar1=pad_total[win][:, r : r + 1],
                        scalar2=inverse[win][:, r : r + 1],
                        op0=ALU.subtract,
                        op1=ALU.mult,
                    )
            else:
                tiles = TILES_PER_WIN - 1 if win == WINDOWS - 1 else TILES_PER_WIN
                nc.vector.tensor_tensor(
                    out=o_sb[:, :tiles, :],
                    in0=o_bank[win][:, :tiles, :],
                    in1=inverse[win][:, :tiles].unsqueeze(2).to_broadcast([P, tiles, FEAT]),
                    op=ALU.mult,
                )
            rows = slice(win * WIN, (win + 1) * WIN)
            dst = out_rows[rows, :].rearrange("(p r) d -> p r d", r=TILES_PER_WIN)
            if win < WINDOWS - 1:
                nc.sync.dma_start(out=dst, in_=o_sb[:])
            else:
                last = TILES_PER_WIN - 1
                nc.sync.dma_start(out=dst[:, :last, :], in_=o_sb[:, :last, :])
                nc.vector.tensor_scalar(
                    out=o_sb[:, last, :],
                    in0=o_bank[WINDOWS][:, :FEAT],
                    scalar1=inverse[win][:, last:],
                    scalar2=None,
                    op0=ALU.mult,
                )
                nc.sync.dma_start(out=dst[:, last:, :], in_=o_sb[:, last:, :])

        def is_tile(i):
            return 0 <= i < TILES

        def window_starting_at(i):
            return i // TILES_PER_WIN if is_tile(i) and i % TILES_PER_WIN == 0 else None

        def preparing(n):
            if n == -1:
                return 1
            return window_starting_at(n + PREP_LEAD) if n > 0 else None

        for win in range(FIRST_LOADS):
            load_window(win)
        regroup_v(0)
        prepare_first_window()
        padding_logit(0)

        for n in range(-2, TILES + 5):
            if window_starting_at(n + LOAD_LEAD) is not None:
                load_window(window_starting_at(n + LOAD_LEAD))

            if is_tile(n + 2):
                scores(n + 2, BACK)
            if is_tile(n):
                exponential(n, BACK)
            if preparing(n) is not None and n > 0:
                transpose_qk(preparing(n))
            if window_starting_at(n - 7) is not None:
                weighted_v(window_starting_at(n - 7))
            if is_tile(n + 2):
                scores(n + 2, CUR)
            if n == -1:
                transpose_qk(preparing(n))
            if is_tile(n):
                exponential(n, CUR)
            if n == TILES:
                regroup_e(n - 1, CUR, CUR, nc.scalar.copy)
            elif is_tile(n - 1):
                regroup_e(n - 1, halves((n - 1) // TILES_PER_WIN)[0], CUR, nc.scalar.copy)
            if is_tile(n):
                transpose_e(n)
            copying = preparing(n - 1)
            if copying is not None and copied_by_scalar(copying):
                copy_qk(copying)

            if is_tile(n + 1):
                row_max(n + 1)
            if n % 2 == 1 and is_tile(n - 3):
                quantise_e((n - 3) // PAIR)
            if window_starting_at(n - 3) is not None:
                quantise_v(window_starting_at(n - 3))
            if window_starting_at(n - 7) is not None:
                invert_sums(window_starting_at(n - 7))
            if is_tile(n + 1):
                exp_bias(n + 1)

            soon = window_starting_at(n + PREP_LEAD + 1)
            if soon is not None and has_padding(soon):
                padding_logit(soon)
            if copying is not None and not copied_by_scalar(copying):
                copy_qk(copying)
            if window_starting_at(n - 5) is not None:
                sum_rows(window_starting_at(n - 5))
            if window_starting_at(n - 8) is not None:
                finish(window_starting_at(n - 8))
            if n == TILES:
                regroup_e(n - 1, BACK, BACK, nc.vector.tensor_copy)
            if n > 0 and window_starting_at(n + 1) is not None:
                regroup_v(window_starting_at(n + 1))
